import numpy as np
import ml_dtypes


def mxq(x, axis, fmt="e4m3"):
    dtype, down = {"e4m3": (ml_dtypes.float8_e4m3fn, 7), "e5m2": (ml_dtypes.float8_e5m2, 14)}[fmt]
    v = np.moveaxis(np.asarray(x, np.float32).astype(ml_dtypes.bfloat16).astype(np.float64), axis, -1)
    blocks = v.reshape(v.shape[:-1] + (-1, 32))
    amax = np.abs(blocks).max(-1, keepdims=True)
    byte = np.maximum(np.where(amax > 0, np.frexp(amax)[1] - 1 + 127, 0) - down, 1)
    scale = np.exp2(byte - 127.0)
    codes = (blocks / scale).astype(np.float32).astype(dtype).astype(np.float64)
    return np.moveaxis((codes * scale).reshape(v.shape), -1, axis)


WIDE = False


def mx_kscale(k):
    if not WIDE:
        return np.ones(k)
    levels = np.array([10, -10, 5, -5, 0])
    if k % 512:
        return np.exp2(np.random.permutation(np.resize(levels, k // 32))).repeat(32)
    a = np.empty((k // 512, 16))
    for p in range(k // 512):
        a[p, :8] = np.random.permutation(np.resize(levels, 8))
        for g in range(8):
            far = levels[np.abs(levels - a[p, g]) >= 10]
            a[p, g + 8] = far[np.random.randint(len(far))]
    return np.exp2(a.ravel()).repeat(32)


BF16 = ml_dtypes.bfloat16


def bf(x):
    return np.asarray(x, np.float32).astype(BF16)


def f64(x):
    return np.asarray(x).astype(np.float64)


B, N, C = 8, 512, 512
R = B * N
G = 3 * C
DENS = 0.1


def setup_inputs():
    s, t = mx_kscale(N), mx_kscale(C)
    edge = np.random.random((B, N, N)) < DENS
    weights = np.where(edge, np.random.random((B, N, N)), 0.0) / np.sqrt(DENS * N / 3.0)
    return {"adjacent": bf(weights * s),
            "annotations": bf(np.random.standard_normal((B, N, C)) / s[:, None] * t),
            "gc_bias": bf(np.random.standard_normal((1, 1, C)) * 0.3 * t),
            "kernel": bf(np.random.standard_normal((C, G)) / np.sqrt(C) / t[:, None]),
            "bias_x": bf(np.random.standard_normal(G) * 0.3)}


def reference(adjacent, annotations, gc_bias, kernel, bias_x):
    a = f64(adjacent)
    v = (mxq(a, a.ndim - 1, "e4m3") @ mxq(f64(annotations), 1, "e4m3")) + f64(gc_bias)
    x = v.reshape(-1, v.shape[-1])
    return (mxq(x, 1, "e4m3") @ mxq(f64(kernel), 0, "e4m3")) + f64(bias_x)

@@ -1,0 +1,352 @@
+from contextlib import ExitStack
+
+import concourse.mybir as mybir
+from concourse.masks import make_identity
+
+F32 = mybir.dt.float32
+BF16 = mybir.dt.bfloat16
+U32 = mybir.dt.uint32
+U8 = mybir.dt.uint8
+FP8X4 = mybir.dt.float8_e4m3fn_x4
+ACT = mybir.ActivationFunctionType
+ALU = mybir.AluOpType
+
+P = 128
+B, N, C, G = 8, 512, 512, 1536
+R = N // P
+M = C // P
+GT = G // 512
+FLOPS = 2 * B * N * N * C + 2 * B * N * C * G
+
+MANUAL = True
+S_BANKS = ((3, 0), (3, 1))
+OV_BUFS = 4
+OS_BUFS = 0
+AT_BUFS = 2
+XR_ON_V = (0, 1)
+K1 = 7
+LOAD_ORDER = ("a0", "g", "x0", "x1", "k", "a1", "a2", "x2", "a3", "x3", "a4", "x4", "a5", "x5", "a6", "x6", "a7", "x7")
+
+
+def tile_gatedgraphconvolution_pa_t_kernel(tc, adjacent, annotations, gc_bias, kernel, bias_x, out):
+    nc = tc.nc
+    with ExitStack() as ctx:
+        if MANUAL:
+            ctx.enter_context(tc.manual_schedule())
+        const = ctx.enter_context(tc.tile_pool(name="const", bufs=1))
+        raw = ctx.enter_context(tc.tile_pool(name="raw", bufs=B))
+        work = ctx.enter_context(tc.tile_pool(name="work", bufs=2))
+        one = ctx.enter_context(tc.tile_pool(name="one", bufs=1))
+        stage = ctx.enter_context(tc.tile_pool(name="stage", bufs=8))
+        ps_s = ctx.enter_context(tc.psum_pool(name="ps_s", bufs=4))
+        ps_ov = ctx.enter_context(tc.psum_pool(name="ps_ov", bufs=OV_BUFS))
+
+        out_v = out.rearrange("(b p r) g -> b r p g", p=P, r=R)
+        T = {}
+
+        def cols(gt):
+            return slice(gt * 512, (gt + 1) * 512)
+
+        def s_banks(b):
+            return S_BANKS if b > 0 else ()
+
+        ident_f32 = const.tile([P, P], F32)
+        make_identity(nc, ident_f32[:])
+        ones = const.tile([P, P], BF16)
+        nc.vector.memset(ones[:], 1.0)
+        gb16 = const.tile([P, M], BF16)
+        brow = const.tile([P, G], BF16)
+        nc.vector.memset(brow[:], 0.0)
+        k_raw = const.tile([P, M, G], BF16)
+        kg = const.tile([P, G, 4], BF16, align_bytes=64)
+        k_codes = const.tile([P, G], U32, align_bytes=64)
+        k_sc = const.tile([P, G], U8, align_bytes=64)
+        gb = const.tile([P, M], F32)
+        bias_bc = const.tile([P, G], F32)
+
+        for what in LOAD_ORDER:
+            if what == "g":
+                nc.sync.dma_start(out=gb16[:], in_=gc_bias.rearrange("a b (p t) -> (a b p) t", t=M))
+                nc.sync.dma_start(out=brow[0:1, :], in_=bias_x.rearrange("(o g) -> o g", o=1))
+            elif what == "k":
+                nc.sync.dma_start(out=k_raw[:], in_=kernel.rearrange("(p j) g -> p j g", j=M))
+            elif what[0] == "a":
+                b = int(what[1])
+                a_raw = raw.tile([P, R * N], BF16)
+                nc.sync.dma_start(out=a_raw[:], in_=adjacent[b].rearrange("(p r) j -> p (r j)", r=R))
+                T[("a_raw", b)] = a_raw
+            else:
+                b = int(what[1])
+                x_raw = raw.tile([P, 4, C], BF16)
+                nc.sync.dma_start(out=x_raw[:], in_=annotations[b].rearrange("(p t) c -> p t c", t=4))
+                T[("x_raw", b)] = x_raw
+
+        def regroup(eng, dst, src):
+            if eng == "G":
+                nc.gpsimd.tensor_scalar(out=dst, in0=src.rearrange("p t c -> p c t"), scalar1=1.0, scalar2=0.0, op0=ALU.mult, op1=ALU.add)
+            elif eng == "V":
+                nc.vector.tensor_copy(out=dst.rearrange("p (c i) t -> p c t i", i=4), in_=src.rearrange("p t (c i) -> p c t i", i=4))
+            else:
+                nc.scalar.copy(out=dst.rearrange("p (c i) t -> p c t i", i=4), in_=src.rearrange("p t (c i) -> p c t i", i=4))
+
+        def biases():
+            nc.scalar.copy(out=gb[:], in_=gb16[:])
+            for gt in range(GT):
+                b_ps = ps_ov.tile([P, 512], F32, tag="ov_ps")
+                nc.tensor.matmul(out=b_ps[:], lhsT=ones[:], rhs=brow[:, cols(gt)], start=True, stop=True)
+                nc.scalar.copy(out=bias_bc[:, cols(gt)], in_=b_ps[:])
+
+        def kr(gt, eng):
+            regroup(eng, kg[:, cols(gt), :], k_raw[:, :, cols(gt)])
+
+        def qk(gt):
+            nc.vector.quantize_mx(out=k_codes[:, cols(gt)].bitcast(FP8X4), scales=k_sc[:, cols(gt)], in_=kg[:, cols(gt), :].rearrange("p c t -> p (c t)"))
+
+        def xr(b):
+            xg = one.tile([P, C, 4], BF16, align_bytes=64)
+            T[("xg", b)] = xg
+            dst = xg[:].rearrange("p (t m) j -> p t m j", t=4)
+            src = T[("x_raw", b)][:].rearrange("p j (m t) -> p t m j", t=4)
+            if b in XR_ON_V:
+                nc.vector.tensor_copy(out=dst, in_=src)
+            else:
+                nc.gpsimd.tensor_scalar(out=dst, in0=src, scalar1=1.0, scalar2=0.0, op0=ALU.mult, op1=ALU.add)
+
+        def tr(b, h):
+            aw = T[("a_raw", b)][:].bitcast(F32).rearrange("p (r q u) -> p r u q", r=R, u=2)
+            at_ps = ps_s.tile([P, 2, 256], F32, tag="s_ps")
+            T[("at", b, h)] = at_ps
+            for rr in range(2):
+                for u in range(2):
+                    nc.tensor.transpose(at_ps[:, u, rr * P:(rr + 1) * P], aw[:, 2 * h + rr, u, :], ident_f32[:])
+
+        def ae(b, h):
+            if h == 0:
+                ag = work.tile([P, 4 * N], BF16, align_bytes=64)
+                T[("ag", b)] = ag
+            ag32 = T[("ag", b)][:].bitcast(F32)
+            nc.scalar.copy(
+                out=ag32[:, h * 512:(h + 1) * 512].rearrange("p (n u) -> p n u", u=2),
+                in_=T[("at", b, h)][:].rearrange("p u n -> p n u"),
+            )
+
+        def qx(b):
+            x_codes = work.tile([P, C], U32, align_bytes=64)
+            x_sc = work.tile([P, C], U8, align_bytes=64)
+            T[("xc", b)] = (x_codes, x_sc)
+            nc.vector.quantize_mx(out=x_codes[:].bitcast(FP8X4), scales=x_sc[:], in_=T[("xg", b)][:].rearrange("p c t -> p (c t)"))
+
+        def qa(b):
+            a_codes = work.tile([P, N], U32, align_bytes=64)
+            a_sc = work.tile([P, N], U8, align_bytes=64)
+            T[("ac", b)] = (a_codes, a_sc)
+            nc.vector.quantize_mx(out=a_codes[:].bitcast(FP8X4), scales=a_sc[:], in_=T[("ag", b)][:])
+
+        def s1(b, m):
+            v_ps = ps_s.tile([P, N], F32, tag="s_ps")
+            T[("v", b, m)] = v_ps
+            xc, xs = T[("xc", b)]
+            ac, asc = T[("ac", b)]
+            nc.tensor.matmul_mx(
+                out=v_ps[:],
+                lhsT=xc[:, m * P:(m + 1) * P].bitcast(FP8X4),
+                lhsT_scale=xs[:, m * P:(m + 1) * P],
+                rhs=ac[:].bitcast(FP8X4),
+                rhs_scale=asc[:],
+                start=True,
+                stop=True,
+            )
+
+        def act(b, m):
+            if m == 0:
+                vpl = work.tile([P, M, N], BF16)
+                T[("vpl", b)] = vpl
+            nc.scalar.activation(out=T[("vpl", b)][:, m, :], in_=T[("v", b, m)][:], func=ACT.Identity, bias=gb[:, m:m + 1], scale=1.0)
+
+        def vr(b):
+            vg = work.tile([P, N, M], BF16, align_bytes=64)
+            T[("vg", b)] = vg
+            regroup("S", vg[:], T[("vpl", b)][:])
+
+        def qv(b):
+            v_codes = work.tile([P, N], U32, align_bytes=64)
+            v_sc = work.tile([P, N], U8, align_bytes=64)
+            T[("vc", b)] = (v_codes, v_sc)
+            nc.vector.quantize_mx(out=v_codes[:].bitcast(FP8X4), scales=v_sc[:], in_=T[("vg", b)][:].rearrange("p c t -> p (c t)"))
+
+        def s2(b, r, gt):
+            if (r, gt) in s_banks(b):
+                os_ps = ps_s.tile([P, 512], F32, tag="s_ps")
+                o_ps = os_ps
+            else:
+                ov_ps = ps_ov.tile([P, 512], F32)
+                o_ps = ov_ps
+            T[("o", b, r, gt)] = o_ps
+            vc, vs = T[("vc", b)]
+            nc.tensor.matmul_mx(
+                out=o_ps[:],
+                lhsT=vc[:, r * P:(r + 1) * P].bitcast(FP8X4),
+                lhsT_scale=vs[:, r * P:(r + 1) * P],
+                rhs=k_codes[:, cols(gt)].bitcast(FP8X4),
+                rhs_scale=k_sc[:, cols(gt)],
+                start=True,
+                stop=True,
+            )
+
+        done = {}
+
+        def leave(b, r, gt):
+            if ("osb", b, r) not in T:
+                osb = stage.tile([P, G], F32)
+                T[("osb", b, r)] = osb
+                done[(b, r)] = 0
+            dst = T[("osb", b, r)][:, cols(gt)]
+            if (r, gt) in s_banks(b):
+                nc.scalar.copy(out=dst, in_=T[("o", b, r, gt)][:])
+                if (r, gt) == s_banks(b)[-1]:
+                    lo, hi = s_banks(b)[0][1] * 512, (gt + 1) * 512
+                    both = T[("osb", b, r)][:, lo:hi]
+                    nc.gpsimd.tensor_tensor(out=both, in0=both, in1=bias_bc[:, lo:hi], op=ALU.add)
+            else:
+                nc.vector.tensor_tensor(out=dst, in0=T[("o", b, r, gt)][:], in1=bias_bc[:, cols(gt)], op=ALU.add)
+            done[(b, r)] += 1
+            if done[(b, r)] == GT:
+                nc.sync.dma_start(out=out_v[b, r], in_=T[("osb", b, r)][:])
+
+        v_stream = [(b, r, gt) for b in range(B) for r in range(R) for gt in range(GT) if (r, gt) not in s_banks(b)]
+        pos = {"pe": 0, "v": 0}
+        quantised = set()
+
+        def fill():
+            while pos["pe"] < min(pos["v"] + OV_BUFS, len(v_stream)) and v_stream[pos["pe"]][0] in quantised:
+                b, r, gt = v_stream[pos["pe"]]
+                s2(b, r, gt)
+                pos["pe"] += 1
+
+        def fa(n):
+            for i in range(n):
+                if pos["v"] < len(v_stream) and v_stream[pos["v"]][0] in quantised:
+                    fill()
+                    b, r, gt = v_stream[pos["v"]]
+                    leave(b, r, gt)
+                    pos["v"] += 1
+                    fill()
+
+        def tr2(b):
+            tr(b, 0)
+            tr(b, 1)
+
+        def ae2(b):
+            ae(b, 0)
+            ae(b, 1)
+
+        def on(b):
+            return 0 <= b < B
+
+        tr2(0)
+        xr(0)
+        ae2(0)
+        qx(0)
+        qa(0)
+        biases()
+        xr(1)
+        s1(0, 0)
+        s1(0, 1)
+        act(0, 0)
+        s1(0, 2)
+        act(0, 1)
+        s1(0, 3)
+        act(0, 2)
+        act(0, 3)
+        for gt in range(GT):
+            kr(gt, "V")
+        for gt in range(GT):
+            qk(gt)
+        tr2(1)
+        vr(0)
+        ae2(1)
+        tr2(2)
+        ae2(2)
+        qv(0)
+        quantised.add(0)
+        fill()
+        qa(1)
+        qa(2)
+        qx(1)
+        xr(2)
+        s1(1, 0)
+        s1(1, 1)
+        fa(1)
+        act(1, 0)
+        s1(1, 2)
+        fa(1)
+        act(1, 1)
+        s1(1, 3)
+        fa(1)
+        act(1, 2)
+        act(1, 3)
+        tr(3, 0)
+        fa(1)
+        tr(3, 1)
+        fa(1)
+        qx(2)
+        xr(3)
+        vr(1)
+        s1(2, 0)
+        s1(2, 1)
+        fa(2)
+        ae2(3)
+        fa(1)
+        act(2, 0)
+        s1(2, 2)
+        fa(1)
+        act(2, 1)
+        s1(2, 3)
+        fa(1)
+        act(2, 2)
+        act(2, 3)
+        fa(1)
+        for j in range(B):
+            if on(j + 1):
+                qv(j + 1)
+                quantised.add(j + 1)
+            if on(j + 3):
+                qa(j + 3)
+                qx(j + 3)
+            fill()
+            if on(j + 4):
+                xr(j + 4)
+            if on(j + 1):
+                for (r, gt) in s_banks(j + 1):
+                    s2(j + 1, r, gt)
+                    leave(j + 1, r, gt)
+                    fa(1)
+            if on(j + 2):
+                vr(j + 2)
+            if on(j + 4):
+                tr(j + 4, 0)
+            fa(1)
+            if on(j + 4):
+                tr(j + 4, 1)
+            fa(1)
+            if on(j + 3):
+                s1(j + 3, 0)
+                s1(j + 3, 1)
+            fa(1)
+            if on(j + 4):
+                ae(j + 4, 0)
+                fa(1)
+                ae(j + 4, 1)
+            fa(1)
+            if on(j + 3):
+                act(j + 3, 0)
+                s1(j + 3, 2)
+                fa(1)
+                act(j + 3, 1)
+                s1(j + 3, 3)
+                fa(1)
+                act(j + 3, 2)
+                fa(1)
+                act(j + 3, 3)
+            target = sum([R * GT - len(s_banks(b)) for b in range(j + 1)]) + (K1 if on(j + 1) else 0)
+            fa(max(0, target - pos["v"]))

@@ -105,8 +105,8 @@ def tile_gatedgraphconvolution_pa_t_kernel(tc, adjacent, annotations, gc_bias, k
         def xr(b):
             xg = one.tile([P, C, 4], BF16, align_bytes=64)
             T[("xg", b)] = xg
-            dst = xg[:].rearrange("p (t m) j -> p t m j", t=4)
-            src = T[("x_raw", b)][:].rearrange("p j (m t) -> p t m j", t=4)
+            dst = xg[:].rearrange("p (t m) j -> p m t j", t=4)
+            src = T[("x_raw", b)][:].rearrange("p j (m t) -> p m t j", t=4)
             if b in XR_ON_V:
                 nc.vector.tensor_copy(out=dst, in_=src)
             else:

@@ -285,10 +285,8 @@ def tile_gatedgraphconvolution_pa_t_kernel(tc, adjacent, annotations, gc_bias, k
         fa(1)
         act(1, 2)
         act(1, 3)
-        tr(3, 0)
-        fa(1)
-        tr(3, 1)
-        fa(1)
+        tr2(3)
+        fa(2)
         qx(2)
         xr(3)
         vr(1)
@@ -324,11 +322,8 @@ def tile_gatedgraphconvolution_pa_t_kernel(tc, adjacent, annotations, gc_bias, k
             if on(j + 2):
                 vr(j + 2)
             if on(j + 4):
-                tr(j + 4, 0)
-            fa(1)
-            if on(j + 4):
-                tr(j + 4, 1)
-            fa(1)
+                tr2(j + 4)
+            fa(2)
             if on(j + 3):
                 s1(j + 3, 0)
                 s1(j + 3, 1)

@@ -25,6 +25,8 @@ OS_BUFS = 0
 AT_BUFS = 2
 XR_ON_V = (0, 1)
 K1 = 7
+WARM_FIRST = 5
+WARM_NEXT = 2
 LOAD_ORDER = ("a0", "g", "x0", "x1", "k", "a1", "a2", "x2", "a3", "x3", "a4", "x4", "a5", "x5", "a6", "x6", "a7", "x7")
 
 
@@ -57,6 +59,8 @@ def tile_gatedgraphconvolution_pa_t_kernel(tc, adjacent, annotations, gc_bias, k
         gb16 = const.tile([P, M], BF16)
         brow = const.tile([P, G], BF16)
         nc.vector.memset(brow[:], 0.0)
+        idle_rhs = const.tile([P, 512], BF16)
+        nc.gpsimd.memset(idle_rhs[:], 0.0)
         k_raw = const.tile([P, M, G], BF16)
         kg = const.tile([P, G, 4], BF16, align_bytes=64)
         k_codes = const.tile([P, G], U32, align_bytes=64)
@@ -88,6 +92,11 @@ def tile_gatedgraphconvolution_pa_t_kernel(tc, adjacent, annotations, gc_bias, k
                 nc.vector.tensor_copy(out=dst.rearrange("p (c i) t -> p c t i", i=4), in_=src.rearrange("p t (c i) -> p c t i", i=4))
             else:
                 nc.scalar.copy(out=dst.rearrange("p (c i) t -> p c t i", i=4), in_=src.rearrange("p t (c i) -> p c t i", i=4))
+
+        def warm(n):
+            for i in range(n):
+                w_ps = ps_ov.tile([P, 512], F32, tag="ov_ps")
+                nc.tensor.matmul(out=w_ps[:], lhsT=ones[:], rhs=idle_rhs[:], start=True, stop=True)
 
         def biases():
             nc.scalar.copy(out=gb[:], in_=gb16[:])
@@ -243,12 +252,14 @@ def tile_gatedgraphconvolution_pa_t_kernel(tc, adjacent, annotations, gc_bias, k
         def on(b):
             return 0 <= b < B
 
+        warm(WARM_FIRST)
         tr2(0)
         xr(0)
         ae2(0)
         qx(0)
         qa(0)
         biases()
+        warm(WARM_NEXT)
         xr(1)
         s1(0, 0)
         s1(0, 1)

@@ -24,7 +24,7 @@ OV_BUFS = 4
 OS_BUFS = 0
 AT_BUFS = 2
 XR_ON_V = (0, 1)
-K1 = 7
+K1 = 9
 WARM_FIRST = 5
 WARM_NEXT = 2
 LOAD_ORDER = ("a0", "g", "x0", "x1", "k", "a1", "a2", "x2", "a3", "x3", "a4", "x4", "a5", "x5", "a6", "x6", "a7", "x7")

@@ -27,7 +27,7 @@ XR_ON_V = (0, 1)
 K1 = 9
 WARM_FIRST = 5
 WARM_NEXT = 2
-LOAD_ORDER = ("a0", "g", "x0", "x1", "k", "a1", "a2", "x2", "a3", "x3", "a4", "x4", "a5", "x5", "a6", "x6", "a7", "x7")
+LOAD_ORDER = ("a0", "x0", "g", "x1", "k", "a1", "a2", "x2", "a3", "x3", "a4", "x4", "a5", "x5", "a6", "x6", "a7", "x7")
 
 
 def tile_gatedgraphconvolution_pa_t_kernel(tc, adjacent, annotations, gc_bias, kernel, bias_x, out):
@@ -52,15 +52,15 @@ def tile_gatedgraphconvolution_pa_t_kernel(tc, adjacent, annotations, gc_bias, k
         def s_banks(b):
             return S_BANKS if b > 0 else ()
 
+        idle_rhs = const.tile([P, 512], BF16)
+        nc.gpsimd.memset(idle_rhs[:], 0.0)
         ident_f32 = const.tile([P, P], F32)
         make_identity(nc, ident_f32[:])
         ones = const.tile([P, P], BF16)
         nc.vector.memset(ones[:], 1.0)
         gb16 = const.tile([P, M], BF16)
         brow = const.tile([P, G], BF16)
-        nc.vector.memset(brow[:], 0.0)
-        idle_rhs = const.tile([P, 512], BF16)
-        nc.gpsimd.memset(idle_rhs[:], 0.0)
+        nc.vector.memset(brow[:].bitcast(F32), 0.0)
         k_raw = const.tile([P, M, G], BF16)
         kg = const.tile([P, G, 4], BF16, align_bytes=64)
         k_codes = const.tile([P, G], U32, align_bytes=64)

@@ -25,9 +25,9 @@ OS_BUFS = 0
 AT_BUFS = 2
 XR_ON_V = (0, 1)
 K1 = 9
-WARM_FIRST = 5
+WARM_FIRST = 3
 WARM_NEXT = 2
-LOAD_ORDER = ("a0", "x0", "g", "x1", "k", "a1", "a2", "x2", "a3", "x3", "a4", "x4", "a5", "x5", "a6", "x6", "a7", "x7")
+LOAD_ORDER = ("a0h", "x0", "g", "x1", "k", "a1", "a2", "x2", "a3", "x3", "a4", "x4", "a5", "x5", "a6", "x6", "a7", "x7")
 
 
 def tile_gatedgraphconvolution_pa_t_kernel(tc, adjacent, annotations, gc_bias, kernel, bias_x, out):
@@ -74,6 +74,12 @@ def tile_gatedgraphconvolution_pa_t_kernel(tc, adjacent, annotations, gc_bias, k
                 nc.sync.dma_start(out=brow[0:1, :], in_=bias_x.rearrange("(o g) -> o g", o=1))
             elif what == "k":
                 nc.sync.dma_start(out=k_raw[:], in_=kernel.rearrange("(p j) g -> p j g", j=M))
+            elif what == "a0h":
+                a_raw = raw.tile([P, R * N], BF16)
+                half = R * N // 2
+                for h in range(2):
+                    nc.sync.dma_start(out=a_raw[:, h * half:(h + 1) * half], in_=adjacent[0].rearrange("(p r) j -> p (r j)", r=R)[:, h * half:(h + 1) * half])
+                T[("a_raw", 0)] = a_raw
             elif what[0] == "a":
                 b = int(what[1])
                 a_raw = raw.tile([P, R * N], BF16)

@@ -66,7 +66,7 @@ def tile_gatedgraphconvolution_pa_t_kernel(tc, adjacent, annotations, gc_bias, k
         k_codes = const.tile([P, G], U32, align_bytes=64)
         k_sc = const.tile([P, G], U8, align_bytes=64)
         gb = const.tile([P, M], F32)
-        bias_bc = const.tile([P, G], F32)
+        bias_bc = const.tile([P, G], BF16)
 
         for what in LOAD_ORDER:
             if what == "g":
@@ -106,10 +106,11 @@ def tile_gatedgraphconvolution_pa_t_kernel(tc, adjacent, annotations, gc_bias, k
 
         def biases():
             nc.scalar.copy(out=gb[:], in_=gb16[:])
-            for gt in range(GT):
-                b_ps = ps_ov.tile([P, 512], F32, tag="ov_ps")
-                nc.tensor.matmul(out=b_ps[:], lhsT=ones[:], rhs=brow[:, cols(gt)], start=True, stop=True)
-                nc.scalar.copy(out=bias_bc[:, cols(gt)], in_=b_ps[:])
+            for lo, hi in ((0, 2), (2, GT)):
+                b_ps = ps_ov.tile([P, (hi - lo) * 512], BF16, tag="ov_ps")
+                for gt in range(lo, hi):
+                    nc.tensor.matmul(out=b_ps[:, (gt - lo) * 512:(gt - lo + 1) * 512], lhsT=ones[:], rhs=brow[:, cols(gt)], start=True, stop=True)
+                nc.scalar.copy(out=bias_bc[:, lo * 512:hi * 512], in_=b_ps[:])
 
         def kr(gt, eng):
             regroup(eng, kg[:, cols(gt), :], k_raw[:, :, cols(gt)])

from contextlib import ExitStack

import concourse.mybir as mybir
from concourse.masks import make_identity

F32 = mybir.dt.float32
BF16 = mybir.dt.bfloat16
U32 = mybir.dt.uint32
U8 = mybir.dt.uint8
FP8X4 = mybir.dt.float8_e4m3fn_x4
ACT = mybir.ActivationFunctionType
ALU = mybir.AluOpType

P = 128
B, N, C, G = 8, 512, 512, 1536
R = N // P
M = C // P
GT = G // 512
FLOPS = 2 * B * N * N * C + 2 * B * N * C * G

MANUAL = True
S_BANKS = ((3, 0), (3, 1))
OV_BUFS = 4
OS_BUFS = 0
AT_BUFS = 2
XR_ON_V = (0, 1)
K1 = 9
WARM_FIRST = 3
WARM_NEXT = 2
LOAD_ORDER = ("a0h", "x0", "g", "x1", "k", "a1", "a2", "x2", "a3", "x3", "a4", "x4", "a5", "x5", "a6", "x6", "a7", "x7")


def tile_gatedgraphconvolution_pa_t_kernel(tc, adjacent, annotations, gc_bias, kernel, bias_x, out):
    nc = tc.nc
    with ExitStack() as ctx:
        if MANUAL:
            ctx.enter_context(tc.manual_schedule())
        const = ctx.enter_context(tc.tile_pool(name="const", bufs=1))
        raw = ctx.enter_context(tc.tile_pool(name="raw", bufs=B))
        work = ctx.enter_context(tc.tile_pool(name="work", bufs=2))
        one = ctx.enter_context(tc.tile_pool(name="one", bufs=1))
        stage = ctx.enter_context(tc.tile_pool(name="stage", bufs=8))
        ps_s = ctx.enter_context(tc.psum_pool(name="ps_s", bufs=4))
        ps_ov = ctx.enter_context(tc.psum_pool(name="ps_ov", bufs=OV_BUFS))

        out_v = out.rearrange("(b p r) g -> b r p g", p=P, r=R)
        T = {}

        def cols(gt):
            return slice(gt * 512, (gt + 1) * 512)

        def s_banks(b):
            return S_BANKS if b > 0 else ()

        idle_rhs = const.tile([P, 512], BF16)
        nc.gpsimd.memset(idle_rhs[:], 0.0)
        ident_f32 = const.tile([P, P], F32)
        make_identity(nc, ident_f32[:])
        ones = const.tile([P, P], BF16)
        nc.vector.memset(ones[:], 1.0)
        gb16 = const.tile([P, M], BF16)
        brow = const.tile([P, G], BF16)
        nc.vector.memset(brow[:].bitcast(F32), 0.0)
        k_raw = const.tile([P, M, G], BF16)
        kg = const.tile([P, G, 4], BF16, align_bytes=64)
        k_codes = const.tile([P, G], U32, align_bytes=64)
        k_sc = const.tile([P, G], U8, align_bytes=64)
        gb = const.tile([P, M], F32)
        bias_bc = const.tile([P, G], BF16)

        for what in LOAD_ORDER:
            if what == "g":
                nc.sync.dma_start(out=gb16[:], in_=gc_bias.rearrange("a b (p t) -> (a b p) t", t=M))
                nc.sync.dma_start(out=brow[0:1, :], in_=bias_x.rearrange("(o g) -> o g", o=1))
            elif what == "k":
                nc.sync.dma_start(out=k_raw[:], in_=kernel.rearrange("(p j) g -> p j g", j=M))
            elif what == "a0h":
                a_raw = raw.tile([P, R * N], BF16)
                half = R * N // 2
                for h in range(2):
                    nc.sync.dma_start(out=a_raw[:, h * half:(h + 1) * half], in_=adjacent[0].rearrange("(p r) j -> p (r j)", r=R)[:, h * half:(h + 1) * half])
                T[("a_raw", 0)] = a_raw
            elif what[0] == "a":
                b = int(what[1])
                a_raw = raw.tile([P, R * N], BF16)
                nc.sync.dma_start(out=a_raw[:], in_=adjacent[b].rearrange("(p r) j -> p (r j)", r=R))
                T[("a_raw", b)] = a_raw
            else:
                b = int(what[1])
                x_raw = raw.tile([P, 4, C], BF16)
                nc.sync.dma_start(out=x_raw[:], in_=annotations[b].rearrange("(p t) c -> p t c", t=4))
                T[("x_raw", b)] = x_raw

        def regroup(eng, dst, src):
            if eng == "G":
                nc.gpsimd.tensor_scalar(out=dst, in0=src.rearrange("p t c -> p c t"), scalar1=1.0, scalar2=0.0, op0=ALU.mult, op1=ALU.add)
            elif eng == "V":
                nc.vector.tensor_copy(out=dst.rearrange("p (c i) t -> p c t i", i=4), in_=src.rearrange("p t (c i) -> p c t i", i=4))
            else:
                nc.scalar.copy(out=dst.rearrange("p (c i) t -> p c t i", i=4), in_=src.rearrange("p t (c i) -> p c t i", i=4))

        def warm(n):
            for i in range(n):
                w_ps = ps_ov.tile([P, 512], F32, tag="ov_ps")
                nc.tensor.matmul(out=w_ps[:], lhsT=ones[:], rhs=idle_rhs[:], start=True, stop=True)

        def biases():
            nc.scalar.copy(out=gb[:], in_=gb16[:])
            for lo, hi in ((0, 2), (2, GT)):
                b_ps = ps_ov.tile([P, (hi - lo) * 512], BF16, tag="ov_ps")
                for gt in range(lo, hi):
                    nc.tensor.matmul(out=b_ps[:, (gt - lo) * 512:(gt - lo + 1) * 512], lhsT=ones[:], rhs=brow[:, cols(gt)], start=True, stop=True)
                nc.scalar.copy(out=bias_bc[:, lo * 512:hi * 512], in_=b_ps[:])

        def kr(gt, eng):
            regroup(eng, kg[:, cols(gt), :], k_raw[:, :, cols(gt)])

        def qk(gt):
            nc.vector.quantize_mx(out=k_codes[:, cols(gt)].bitcast(FP8X4), scales=k_sc[:, cols(gt)], in_=kg[:, cols(gt), :].rearrange("p c t -> p (c t)"))

        def xr(b):
            xg = one.tile([P, C, 4], BF16, align_bytes=64)
            T[("xg", b)] = xg
            dst = xg[:].rearrange("p (t m) j -> p m t j", t=4)
            src = T[("x_raw", b)][:].rearrange("p j (m t) -> p m t j", t=4)
            if b in XR_ON_V:
                nc.vector.tensor_copy(out=dst, in_=src)
            else:
                nc.gpsimd.tensor_scalar(out=dst, in0=src, scalar1=1.0, scalar2=0.0, op0=ALU.mult, op1=ALU.add)

        def tr(b, h):
            aw = T[("a_raw", b)][:].bitcast(F32).rearrange("p (r q u) -> p r u q", r=R, u=2)
            at_ps = ps_s.tile([P, 2, 256], F32, tag="s_ps")
            T[("at", b, h)] = at_ps
            for rr in range(2):
                for u in range(2):
                    nc.tensor.transpose(at_ps[:, u, rr * P:(rr + 1) * P], aw[:, 2 * h + rr, u, :], ident_f32[:])

        def ae(b, h):
            if h == 0:
                ag = work.tile([P, 4 * N], BF16, align_bytes=64)
                T[("ag", b)] = ag
            ag32 = T[("ag", b)][:].bitcast(F32)
            nc.scalar.copy(
                out=ag32[:, h * 512:(h + 1) * 512].rearrange("p (n u) -> p n u", u=2),
                in_=T[("at", b, h)][:].rearrange("p u n -> p n u"),
            )

        def qx(b):
            x_codes = work.tile([P, C], U32, align_bytes=64)
            x_sc = work.tile([P, C], U8, align_bytes=64)
            T[("xc", b)] = (x_codes, x_sc)
            nc.vector.quantize_mx(out=x_codes[:].bitcast(FP8X4), scales=x_sc[:], in_=T[("xg", b)][:].rearrange("p c t -> p (c t)"))

        def qa(b):
            a_codes = work.tile([P, N], U32, align_bytes=64)
            a_sc = work.tile([P, N], U8, align_bytes=64)
            T[("ac", b)] = (a_codes, a_sc)
            nc.vector.quantize_mx(out=a_codes[:].bitcast(FP8X4), scales=a_sc[:], in_=T[("ag", b)][:])

        def s1(b, m):
            v_ps = ps_s.tile([P, N], F32, tag="s_ps")
            T[("v", b, m)] = v_ps
            xc, xs = T[("xc", b)]
            ac, asc = T[("ac", b)]
            nc.tensor.matmul_mx(
                out=v_ps[:],
                lhsT=xc[:, m * P:(m + 1) * P].bitcast(FP8X4),
                lhsT_scale=xs[:, m * P:(m + 1) * P],
                rhs=ac[:].bitcast(FP8X4),
                rhs_scale=asc[:],
                start=True,
                stop=True,
            )

        def act(b, m):
            if m == 0:
                vpl = work.tile([P, M, N], BF16)
                T[("vpl", b)] = vpl
            nc.scalar.activation(out=T[("vpl", b)][:, m, :], in_=T[("v", b, m)][:], func=ACT.Identity, bias=gb[:, m:m + 1], scale=1.0)

        def vr(b):
            vg = work.tile([P, N, M], BF16, align_bytes=64)
            T[("vg", b)] = vg
            regroup("S", vg[:], T[("vpl", b)][:])

        def qv(b):
            v_codes = work.tile([P, N], U32, align_bytes=64)
            v_sc = work.tile([P, N], U8, align_bytes=64)
            T[("vc", b)] = (v_codes, v_sc)
            nc.vector.quantize_mx(out=v_codes[:].bitcast(FP8X4), scales=v_sc[:], in_=T[("vg", b)][:].rearrange("p c t -> p (c t)"))

        def s2(b, r, gt):
            if (r, gt) in s_banks(b):
                os_ps = ps_s.tile([P, 512], F32, tag="s_ps")
                o_ps = os_ps
            else:
                ov_ps = ps_ov.tile([P, 512], F32)
                o_ps = ov_ps
            T[("o", b, r, gt)] = o_ps
            vc, vs = T[("vc", b)]
            nc.tensor.matmul_mx(
                out=o_ps[:],
                lhsT=vc[:, r * P:(r + 1) * P].bitcast(FP8X4),
                lhsT_scale=vs[:, r * P:(r + 1) * P],
                rhs=k_codes[:, cols(gt)].bitcast(FP8X4),
                rhs_scale=k_sc[:, cols(gt)],
                start=True,
                stop=True,
            )

        done = {}

        def leave(b, r, gt):
            if ("osb", b, r) not in T:
                osb = stage.tile([P, G], F32)
                T[("osb", b, r)] = osb
                done[(b, r)] = 0
            dst = T[("osb", b, r)][:, cols(gt)]
            if (r, gt) in s_banks(b):
                nc.scalar.copy(out=dst, in_=T[("o", b, r, gt)][:])
                if (r, gt) == s_banks(b)[-1]:
                    lo, hi = s_banks(b)[0][1] * 512, (gt + 1) * 512
                    both = T[("osb", b, r)][:, lo:hi]
                    nc.gpsimd.tensor_tensor(out=both, in0=both, in1=bias_bc[:, lo:hi], op=ALU.add)
            else:
                nc.vector.tensor_tensor(out=dst, in0=T[("o", b, r, gt)][:], in1=bias_bc[:, cols(gt)], op=ALU.add)
            done[(b, r)] += 1
            if done[(b, r)] == GT:
                nc.sync.dma_start(out=out_v[b, r], in_=T[("osb", b, r)][:])

        v_stream = [(b, r, gt) for b in range(B) for r in range(R) for gt in range(GT) if (r, gt) not in s_banks(b)]
        pos = {"pe": 0, "v": 0}
        quantised = set()

        def fill():
            while pos["pe"] < min(pos["v"] + OV_BUFS, len(v_stream)) and v_stream[pos["pe"]][0] in quantised:
                b, r, gt = v_stream[pos["pe"]]
                s2(b, r, gt)
                pos["pe"] += 1

        def fa(n):
            for i in range(n):
                if pos["v"] < len(v_stream) and v_stream[pos["v"]][0] in quantised:
                    fill()
                    b, r, gt = v_stream[pos["v"]]
                    leave(b, r, gt)
                    pos["v"] += 1
                    fill()

        def tr2(b):
            tr(b, 0)
            tr(b, 1)

        def ae2(b):
            ae(b, 0)
            ae(b, 1)

        def on(b):
            return 0 <= b < B

        warm(WARM_FIRST)
        tr2(0)
        xr(0)
        ae2(0)
        qx(0)
        qa(0)
        biases()
        warm(WARM_NEXT)
        xr(1)
        s1(0, 0)
        s1(0, 1)
        act(0, 0)
        s1(0, 2)
        act(0, 1)
        s1(0, 3)
        act(0, 2)
        act(0, 3)
        for gt in range(GT):
            kr(gt, "V")
        for gt in range(GT):
            qk(gt)
        tr2(1)
        vr(0)
        ae2(1)
        tr2(2)
        ae2(2)
        qv(0)
        quantised.add(0)
        fill()
        qa(1)
        qa(2)
        qx(1)
        xr(2)
        s1(1, 0)
        s1(1, 1)
        fa(1)
        act(1, 0)
        s1(1, 2)
        fa(1)
        act(1, 1)
        s1(1, 3)
        fa(1)
        act(1, 2)
        act(1, 3)
        tr2(3)
        fa(2)
        qx(2)
        xr(3)
        vr(1)
        s1(2, 0)
        s1(2, 1)
        fa(2)
        ae2(3)
        fa(1)
        act(2, 0)
        s1(2, 2)
        fa(1)
        act(2, 1)
        s1(2, 3)
        fa(1)
        act(2, 2)
        act(2, 3)
        fa(1)
        for j in range(B):
            if on(j + 1):
                qv(j + 1)
                quantised.add(j + 1)
            if on(j + 3):
                qa(j + 3)
                qx(j + 3)
            fill()
            if on(j + 4):
                xr(j + 4)
            if on(j + 1):
                for (r, gt) in s_banks(j + 1):
                    s2(j + 1, r, gt)
                    leave(j + 1, r, gt)
                    fa(1)
            if on(j + 2):
                vr(j + 2)
            if on(j + 4):
                tr2(j + 4)
            fa(2)
            if on(j + 3):
                s1(j + 3, 0)
                s1(j + 3, 1)
            fa(1)
            if on(j + 4):
                ae(j + 4, 0)
                fa(1)
                ae(j + 4, 1)
            fa(1)
            if on(j + 3):
                act(j + 3, 0)
                s1(j + 3, 2)
                fa(1)
                act(j + 3, 1)
                s1(j + 3, 3)
                fa(1)
                act(j + 3, 2)
                fa(1)
                act(j + 3, 3)
            target = sum([R * GT - len(s_banks(b)) for b in range(j + 1)]) + (K1 if on(j + 1) else 0)
            fa(max(0, target - pos["v"]))
